import numpy as np
import ml_dtypes


def mxq(x, axis, fmt="e4m3"):
    dtype, down = {"e4m3": (ml_dtypes.float8_e4m3fn, 7), "e5m2": (ml_dtypes.float8_e5m2, 14)}[fmt]
    v = np.moveaxis(np.asarray(x, np.float32).astype(ml_dtypes.bfloat16).astype(np.float64), axis, -1)
    blocks = v.reshape(v.shape[:-1] + (-1, 32))
    amax = np.abs(blocks).max(-1, keepdims=True)
    byte = np.maximum(np.where(amax > 0, np.frexp(amax)[1] - 1 + 127, 0) - down, 1)
    scale = np.exp2(byte - 127.0)
    codes = (blocks / scale).astype(np.float32).astype(dtype).astype(np.float64)
    return np.moveaxis((codes * scale).reshape(v.shape), -1, axis)


WIDE = False


def mx_kscale(k):
    if not WIDE:
        return np.ones(k)
    levels = np.array([10, -10, 5, -5, 0])
    if k % 512:
        return np.exp2(np.random.permutation(np.resize(levels, k // 32))).repeat(32)
    a = np.empty((k // 512, 16))
    for p in range(k // 512):
        a[p, :8] = np.random.permutation(np.resize(levels, 8))
        for g in range(8):
            far = levels[np.abs(levels - a[p, g]) >= 10]
            a[p, g + 8] = far[np.random.randint(len(far))]
    return np.exp2(a.ravel()).repeat(32)


BF16 = ml_dtypes.bfloat16


def bf(x):
    return np.asarray(x, np.float32).astype(BF16)


def f64(x):
    return np.asarray(x).astype(np.float64)


B, S, DIM, N_HEADS, HEAD_DIM, F = 4, 2048, 512, 2, 64, 4096
QD = N_HEADS * HEAD_DIM
THETA = 10000.0
EPS = 1e-6


def rms_norm(x, w):
    return x * (1.0 / np.sqrt(np.mean(x * x, axis=-1, keepdims=True) + EPS)) * w


def rope_tables():
    inv = 1.0 / THETA ** (np.arange(0, HEAD_DIM, 2) / HEAD_DIM)
    freqs = np.outer(np.arange(S), inv)
    return np.cos(freqs), np.sin(freqs)


def rot(u, cos, sin):
    c = cos[None, :, None, :]
    s = sin[None, :, None, :]
    ur, ui = u[..., 0::2], u[..., 1::2]
    yr = ur * c - ui * s
    yi = ur * s + ui * c
    return np.stack([yr, yi], axis=-1).reshape(u.shape)


def setup_inputs():
    s = mx_kscale(DIM)
    sc = 1.0 / np.sqrt(DIM)
    quiet = np.where(np.random.random((B, S, 1)) < 0.125, 1e-3, 1.0)
    return {"x": bf(np.random.standard_normal((B, S, DIM)) * quiet),
            "attn_norm_w": bf((1.0 + 0.1 * np.random.standard_normal(DIM)) * s),
            "wq": bf(np.random.standard_normal((DIM, QD)) * sc / s[:, None]),
            "wk": bf(np.random.standard_normal((DIM, QD)) * sc / s[:, None]),
            "wv": bf(np.random.standard_normal((DIM, QD)) * sc / s[:, None])}


def reference(x, attn_norm_w, wq, wk, wv):
    h = rms_norm(f64(x), f64(attn_norm_w))
    hq = mxq(h, 2, "e4m3")
    q = (hq @ mxq(f64(wq), 0, "e4m3")).reshape(B, S, N_HEADS, HEAD_DIM)
    k = (hq @ mxq(f64(wk), 0, "e4m3")).reshape(B, S, N_HEADS, HEAD_DIM)
    v = (hq @ mxq(f64(wv), 0, "e4m3")).reshape(B, S, N_HEADS, HEAD_DIM)
    cos, sin = rope_tables()
    q = rot(q, cos, sin)
    k = rot(k, cos, sin)
    return q.transpose(0, 2, 1, 3), k.transpose(0, 2, 1, 3), v.transpose(0, 2, 1, 3)

@@ -1,0 +1,306 @@
+import math
+from contextlib import ExitStack
+
+import concourse.masks as masks
+import concourse.mybir as mybir
+
+F32 = mybir.dt.float32
+BF16 = mybir.dt.bfloat16
+U32 = mybir.dt.uint32
+U8 = mybir.dt.uint8
+FP8X4 = mybir.dt.float8_e4m3fn_x4
+ALU = mybir.AluOpType
+ACT = mybir.ActivationFunctionType
+
+P = 128
+BATCH, SEQ, DIM = 4, 2048, 512
+HEADS, HEAD_DIM = 2, 64
+QD = HEADS * HEAD_DIM
+PAIRS = HEAD_DIM // 2
+THETA = 10000.0
+EPS = 1e-6
+
+PACK = 4
+TILES = SEQ // P
+GROUP = 4
+GROUPS = TILES // GROUP
+ROT = 4 * QD
+W_COLS = ROT + QD
+
+ROUND_MAGIC = 1.5 * 2.0**23
+TURN_GRID = 2.0**15
+
+FLOPS = 2 * BATCH * SEQ * DIM * 3 * QD
+
+
+def rotation_turns(nc, work):
+    position = work.tile([P, TILES], F32)
+    nc.gpsimd.iota(
+        position[:], pattern=[[1, TILES]], base=0, channel_multiplier=TILES,
+        allow_small_or_imprecise_dtypes=True,
+    )
+    turns_hi = work.tile([P, TILES, PAIRS], F32)
+    turns_lo = work.tile([P, TILES, PAIRS], F32)
+    for j in range(PAIRS):
+        step = THETA ** (-j / PAIRS) / (2.0 * math.pi)
+        step_hi = round(step * TURN_GRID) / TURN_GRID
+        nc.vector.tensor_scalar_mul(out=turns_hi[:, :, j], in0=position[:], scalar1=step_hi)
+        nc.scalar.mul(out=turns_lo[:, :, j], in_=position[:], mul=step - step_hi)
+
+    whole = work.tile([P, TILES, PAIRS], F32)
+    nc.vector.tensor_scalar(
+        out=whole[:], in0=turns_hi[:], scalar1=ROUND_MAGIC, scalar2=ROUND_MAGIC,
+        op0=ALU.add, op1=ALU.subtract,
+    )
+    nc.vector.tensor_sub(out=turns_hi[:], in0=turns_hi[:], in1=whole[:])
+
+    turns = work.tile([P, TILES, 2, PAIRS], F32)
+    nc.vector.tensor_add(out=turns[:, :, 1, :], in0=turns_hi[:], in1=turns_lo[:])
+    nc.vector.tensor_scalar_add(out=turns[:, :, 0, :], in0=turns[:, :, 1, :], scalar1=0.25)
+    nearest = work.tile([P, TILES, 2, PAIRS], F32)
+    nc.vector.tensor_scalar(
+        out=nearest[:], in0=turns[:], scalar1=ROUND_MAGIC, scalar2=ROUND_MAGIC,
+        op0=ALU.add, op1=ALU.subtract,
+    )
+    nc.vector.tensor_sub(out=turns[:], in0=turns[:], in1=nearest[:])
+    return turns
+
+
+def rotation_table(nc, consts, work, turns):
+    trig = work.tile([P, TILES * 2 * PAIRS], F32)
+    nc.scalar.activation(
+        out=trig[:], in_=turns[:].rearrange("p i c j -> p (i c j)"), func=ACT.Sin,
+        scale=2.0 * math.pi,
+    )
+    table = consts.tile([P, TILES, 2, HEAD_DIM], F32)
+    nc.gpsimd.tensor_scalar(
+        out=table[:].rearrange("p i c (j r) -> p (i c j) r", r=2),
+        in0=trig[:].unsqueeze(2).to_broadcast([P, TILES * 2 * PAIRS, 2]),
+        scalar1=1.0, scalar2=0.0, op0=ALU.mult, op1=ALU.add,
+    )
+    return table
+
+
+def load_weights(nc, work, wq, wk, wv):
+    raw = work.tile([P, 3, PACK, QD], BF16)
+    for m, w in enumerate((wq, wk, wv)):
+        nc.sync.dma_start(
+            out=raw[:, m],
+            in_=w.rearrange("(p t) c -> p t c", t=PACK),
+        )
+    return raw
+
+
+def quantise_weights(nc, consts, work, raw):
+    grouped = work.tile([P, W_COLS, PACK], BF16, align_bytes=64)
+    nc.vector.tensor_copy(
+        out=grouped[:, 0 : 2 * QD, :].rearrange("p (m c) t -> p m c t", m=2),
+        in_=raw[:, 0:2].rearrange("p m t c -> p m c t"),
+    )
+    partner = grouped[:, 2 * QD : ROT, :].rearrange("p (m j r) t -> p m j r t", m=2, r=2)
+    pairs = raw[:, 0:2].rearrange("p m t (j r) -> p m j r t", r=2)
+    nc.vector.tensor_scalar_mul(out=partner[:, :, :, 0, :], in0=pairs[:, :, :, 1, :], scalar1=-1.0)
+    nc.vector.tensor_copy(out=partner[:, :, :, 1, :], in_=pairs[:, :, :, 0, :])
+    nc.vector.tensor_copy(out=grouped[:, ROT:W_COLS, :], in_=raw[:, 2].rearrange("p t c -> p c t"))
+
+    codes = consts.tile([P, W_COLS], U32, align_bytes=64)
+    scales = consts.tile([P, W_COLS], U8, align_bytes=64)
+    for cols in (slice(0, ROT), slice(ROT, W_COLS)):
+        nc.vector.quantize_mx(
+            out=codes[:, cols].bitcast(FP8X4),
+            scales=scales[:, cols],
+            in_=grouped[:, cols, :].rearrange("p c t -> p (c t)"),
+        )
+    return codes, scales
+
+
+def tile_flexattentionblock_pa_t_kernel(tc, x, attn_norm_w, wq, wk, wv, out_0, out_1, out_2):
+    nc = tc.nc
+    n_groups = BATCH * GROUPS
+    with ExitStack() as ctx:
+        consts = ctx.enter_context(tc.tile_pool(name="consts", bufs=1))
+        setup = ctx.enter_context(tc.tile_pool(name="setup", bufs=1))
+        resident = ctx.enter_context(tc.tile_pool(name="resident", bufs=1))
+        stream = ctx.enter_context(tc.tile_pool(name="stream", bufs=3))
+        per_tile = ctx.enter_context(tc.tile_pool(name="per_tile", bufs=GROUP))
+        psum_gain = ctx.enter_context(tc.psum_pool(name="psum_gain", bufs=1))
+        psum_t = ctx.enter_context(tc.psum_pool(name="psum_t", bufs=2))
+        psum_rot = ctx.enter_context(tc.psum_pool(name="psum_rot", bufs=GROUP))
+        psum_v = ctx.enter_context(tc.psum_pool(name="psum_v", bufs=1))
+        ctx.enter_context(tc.manual_schedule())
+
+        zero_col = setup.tile([P, 1], F32)
+        nc.vector.memset(zero_col[:], 0.0)
+        nc.scalar.activation(out=zero_col[:], in_=zero_col[:], func=ACT.Sin)
+
+        gain_row = setup.tile([P, DIM], BF16)
+        nc.vector.memset(gain_row[:], 0.0)
+        x_groups = []
+        for b in range(BATCH):
+            tokens = x[b].rearrange("(p i) k -> p i k", i=TILES)
+            for g in range(GROUPS):
+                x_sb = resident.tile([P, GROUP, DIM], BF16, name="x_%d_%d" % (b, g))
+                nc.sync.dma_start(out=x_sb[:], in_=tokens[:, g * GROUP : (g + 1) * GROUP, :])
+                x_groups.append(x_sb)
+                if b == 0 and g == 0:
+                    nc.sync.dma_start(
+                        out=gain_row[0:1, :], in_=attn_norm_w.rearrange("(o k) -> o k", o=1)
+                    )
+                    w_raw = load_weights(nc, setup, wq, wk, wv)
+
+        turns = rotation_turns(nc, setup)
+        identity = consts.tile([P, P], F32)
+        masks.make_identity(nc, identity[:])
+        minus_half = consts.tile([P, GROUP], F32)
+        nc.gpsimd.memset(minus_half[:], -0.5)
+
+        ones = setup.tile([P, P], BF16)
+        nc.vector.memset(ones[:], 1.0)
+        gain = psum_gain.tile([P, DIM], F32)
+        nc.tensor.matmul(out=gain[:], lhsT=ones[:], rhs=gain_row[:], start=True, stop=True)
+        w_codes, w_scales = quantise_weights(nc, consts, setup, w_raw)
+
+        squares_of, rstd_of, h_of, grouped_of, codes_of = {}, {}, {}, {}, {}
+        v_bank_of, rot_banks_of = {}, {}
+
+        def sum_squares(n, half):
+            if half == 0:
+                squares = stream.tile([P, GROUP], F32)
+                squares_of[n] = squares
+            for t in (2 * half, 2 * half + 1):
+                unread = per_tile.tile([P, DIM], BF16)
+                nc.scalar.activation(
+                    out=unread[:], in_=x_groups[n][:, t, :], func=ACT.Square,
+                    accum_out=squares_of[n][:, t : t + 1],
+                )
+
+        def finish_rstd(n):
+            mean_sq = stream.tile([P, GROUP], F32)
+            nc.gpsimd.tensor_scalar(
+                out=mean_sq[:], in0=squares_of[n][:], scalar1=1.0 / DIM, scalar2=EPS,
+                op0=ALU.mult, op1=ALU.add,
+            )
+            rstd = stream.tile([P, GROUP], F32)
+            nc.gpsimd.tensor_tensor(out=rstd[:], in0=mean_sq[:], in1=minus_half[:], op=ALU.pow)
+            rstd_of[n] = rstd
+
+        def scale_and_turn(n, half):
+            if half == 0:
+                h = stream.tile([P, GROUP, DIM], BF16)
+                grouped = stream.tile([P, GROUP * P * PACK], BF16, align_bytes=64)
+                h_of[n], grouped_of[n] = h, grouped
+            h = h_of[n]
+            for t in (2 * half, 2 * half + 1):
+                nc.vector.scalar_tensor_tensor(
+                    out=h[:, t, :], in0=x_groups[n][:, t, :], scalar=rstd_of[n][:, t : t + 1],
+                    in1=gain[:], op0=ALU.mult, op1=ALU.mult,
+                )
+            turned = psum_t.tile([P, 2, 2 * P], F32)
+            for s in range(2):
+                words = h[:, 2 * half + s, :].bitcast(F32)
+                for u in range(2):
+                    nc.tensor.transpose(
+                        out=turned[:, u, s * P : (s + 1) * P],
+                        in_=words[:, u : 2 * P : 2],
+                        identity=identity[:],
+                    )
+            grouped_words = grouped_of[n][:].bitcast(F32).rearrange("p (r u) -> p r u", u=2)
+            nc.scalar.copy(
+                out=grouped_words[:, half * 2 * P : (half + 1) * 2 * P, :],
+                in_=turned[:].rearrange("p u r -> p r u"),
+            )
+
+        def quantise(n):
+            h_codes = stream.tile([P, GROUP * P], U32, align_bytes=64)
+            h_scales = stream.tile([P, GROUP * P], U8, align_bytes=64)
+            nc.vector.quantize_mx(
+                out=h_codes[:].bitcast(FP8X4), scales=h_scales[:], in_=grouped_of[n][:]
+            )
+            codes_of[n] = (h_codes, h_scales)
+
+        def project_v(n):
+            h_codes, h_scales = codes_of[n]
+            v_ps = psum_v.tile([P, GROUP, QD], F32)
+            for t in range(GROUP):
+                cols = slice(t * P, (t + 1) * P)
+                nc.tensor.matmul_mx(
+                    out=v_ps[:, t, :],
+                    lhsT=h_codes[:, cols].bitcast(FP8X4), lhsT_scale=h_scales[:, cols],
+                    rhs=w_codes[:, ROT:W_COLS].bitcast(FP8X4), rhs_scale=w_scales[:, ROT:W_COLS],
+                    start=True, stop=True,
+                )
+            v_bank_of[n] = v_ps
+
+        def project_rot(n):
+            h_codes, h_scales = codes_of[n]
+            rot_banks = []
+            for t in range(GROUP):
+                cols = slice(t * P, (t + 1) * P)
+                rot_ps = psum_rot.tile([P, ROT], F32)
+                nc.tensor.matmul_mx(
+                    out=rot_ps[:],
+                    lhsT=h_codes[:, cols].bitcast(FP8X4), lhsT_scale=h_scales[:, cols],
+                    rhs=w_codes[:, 0:ROT].bitcast(FP8X4), rhs_scale=w_scales[:, 0:ROT],
+                    start=True, stop=True,
+                )
+                rot_banks.append(rot_ps)
+            rot_banks_of[n] = rot_banks
+
+        def store(n, dram, sb):
+            b, g = divmod(n, GROUPS)
+            rows = dram[b].rearrange("h (p i) d -> p h i d", i=TILES)
+            nc.sync.dma_start(out=rows[:, :, g * GROUP : (g + 1) * GROUP, :], in_=sb)
+
+        def store_v(n):
+            v_sb = stream.tile([P, HEADS, GROUP, HEAD_DIM], F32)
+            nc.scalar.copy(
+                out=v_sb[:], in_=v_bank_of[n][:].rearrange("p t (h d) -> p h t d", h=HEADS)
+            )
+            store(n, out_2, v_sb[:])
+
+        def rotate_and_store(n):
+            first_tile = (n % GROUPS) * GROUP
+            rotated = stream.tile([P, 2 * HEADS, GROUP, HEAD_DIM], F32)
+            for t in range(GROUP):
+                products = per_tile.tile([P, 2, 2 * HEADS, HEAD_DIM], F32)
+                nc.vector.tensor_tensor(
+                    out=products[:],
+                    in0=rot_banks_of[n][t][:].rearrange("p (c r d) -> p c r d", c=2, r=2 * HEADS),
+                    in1=table[:, first_tile + t].unsqueeze(2).to_broadcast(
+                        [P, 2, 2 * HEADS, HEAD_DIM]
+                    ),
+                    op=ALU.mult,
+                )
+                nc.gpsimd.tensor_tensor(
+                    out=rotated[:, :, t, :], in0=products[:, 0], in1=products[:, 1], op=ALU.add
+                )
+            store(n, out_0, rotated[:, 0:HEADS])
+            store(n, out_1, rotated[:, HEADS:])
+
+        for n in range(2):
+            sum_squares(n, 0)
+            sum_squares(n, 1)
+            finish_rstd(n)
+        table = rotation_table(nc, consts, setup, turns)
+
+        for n in range(n_groups + 2):
+            ahead, behind, last = n + 2, n - 1, n - 2
+            if ahead < n_groups:
+                sum_squares(ahead, 0)
+            if n < n_groups:
+                scale_and_turn(n, 0)
+            if 0 <= behind < n_groups:
+                quantise(behind)
+            if ahead < n_groups:
+                sum_squares(ahead, 1)
+            if n < n_groups:
+                scale_and_turn(n, 1)
+            if 0 <= behind < n_groups:
+                project_v(behind)
+                store_v(behind)
+            if last >= 0:
+                rotate_and_store(last)
+            if 0 <= behind < n_groups:
+                project_rot(behind)
+            if ahead < n_groups:
+                finish_rstd(ahead)

@@ -17,6 +17,8 @@ BATCH, SEQ, DIM = 4, 2048, 512
 HEADS, HEAD_DIM = 2, 64
 QD = HEADS * HEAD_DIM
 PAIRS = HEAD_DIM // 2
+ROT_HEADS = 2 * HEADS
+HALF = ROT_HEADS * PAIRS
 THETA = 10000.0
 EPS = 1e-6
 
@@ -24,8 +26,10 @@ PACK = 4
 TILES = SEQ // P
 GROUP = 4
 GROUPS = TILES // GROUP
-ROT = 4 * QD
-W_COLS = ROT + QD
+PAIR = 2
+B_COLS, A_COLS, V_COLS = slice(0, HALF), slice(HALF, 2 * HALF), slice(2 * HALF, 2 * HALF + QD)
+BA_COLS = slice(0, 2 * HALF)
+W_COLS = 2 * HALF + QD
 
 ROUND_MAGIC = 1.5 * 2.0**23
 TURN_GRID = 2.0**15
@@ -54,10 +58,10 @@ def rotation_turns(nc, work):
     )
     nc.vector.tensor_sub(out=turns_hi[:], in0=turns_hi[:], in1=whole[:])
 
-    turns = work.tile([P, TILES, 2, PAIRS], F32)
-    nc.vector.tensor_add(out=turns[:, :, 1, :], in0=turns_hi[:], in1=turns_lo[:])
-    nc.vector.tensor_scalar_add(out=turns[:, :, 0, :], in0=turns[:, :, 1, :], scalar1=0.25)
-    nearest = work.tile([P, TILES, 2, PAIRS], F32)
+    turns = work.tile([P, 2, TILES, PAIRS], F32)
+    nc.vector.tensor_add(out=turns[:, 0], in0=turns_hi[:], in1=turns_lo[:])
+    nc.vector.tensor_scalar_add(out=turns[:, 1], in0=turns[:, 0], scalar1=0.25)
+    nearest = work.tile([P, 2, TILES, PAIRS], F32)
     nc.vector.tensor_scalar(
         out=nearest[:], in0=turns[:], scalar1=ROUND_MAGIC, scalar2=ROUND_MAGIC,
         op0=ALU.add, op1=ALU.subtract,
@@ -66,46 +70,51 @@ def rotation_turns(nc, work):
     return turns
 
 
-def rotation_table(nc, consts, work, turns):
-    trig = work.tile([P, TILES * 2 * PAIRS], F32)
-    nc.scalar.activation(
-        out=trig[:], in_=turns[:].rearrange("p i c j -> p (i c j)"), func=ACT.Sin,
-        scale=2.0 * math.pi,
+def rotation_tables(nc, consts, work, turns):
+    size = TILES * PAIRS
+    cos_table = consts.tile([P, TILES, PAIRS], F32)
+    minus_cos = work.tile([P, size], F32)
+    signed_sin = work.tile([P, 2, size], F32)
+    for out, part, sign in (
+        (cos_table[:].rearrange("p i j -> p (i j)"), 1, 1.0),
+        (minus_cos[:], 1, -1.0),
+        (signed_sin[:, 0], 0, -1.0),
+        (signed_sin[:, 1], 0, 1.0),
+    ):
+        nc.scalar.activation(
+            out=out, in_=turns[:, part].rearrange("p i j -> p (i j)"), func=ACT.Sin,
+            scale=sign * 2.0 * math.pi,
+        )
+    swing_table = consts.tile([P, TILES, PAIRS, 2], F32)
+    nc.gpsimd.tensor_tensor(
+        out=swing_table[:].rearrange("p i j r -> p (i j) r"),
+        in0=minus_cos[:].unsqueeze(2).to_broadcast([P, size, 2]),
+        in1=signed_sin[:].rearrange("p r n -> p n r"),
+        op=ALU.add,
     )
-    table = consts.tile([P, TILES, 2, HEAD_DIM], F32)
-    nc.gpsimd.tensor_scalar(
-        out=table[:].rearrange("p i c (j r) -> p (i c j) r", r=2),
-        in0=trig[:].unsqueeze(2).to_broadcast([P, TILES * 2 * PAIRS, 2]),
-        scalar1=1.0, scalar2=0.0, op0=ALU.mult, op1=ALU.add,
-    )
-    return table
+    return cos_table, swing_table
 
 
 def load_weights(nc, work, wq, wk, wv):
     raw = work.tile([P, 3, PACK, QD], BF16)
     for m, w in enumerate((wq, wk, wv)):
-        nc.sync.dma_start(
-            out=raw[:, m],
-            in_=w.rearrange("(p t) c -> p t c", t=PACK),
-        )
+        nc.sync.dma_start(out=raw[:, m], in_=w.rearrange("(p t) c -> p t c", t=PACK))
     return raw
 
 
 def quantise_weights(nc, consts, work, raw):
     grouped = work.tile([P, W_COLS, PACK], BF16, align_bytes=64)
-    nc.vector.tensor_copy(
-        out=grouped[:, 0 : 2 * QD, :].rearrange("p (m c) t -> p m c t", m=2),
-        in_=raw[:, 0:2].rearrange("p m t c -> p m c t"),
-    )
-    partner = grouped[:, 2 * QD : ROT, :].rearrange("p (m j r) t -> p m j r t", m=2, r=2)
-    pairs = raw[:, 0:2].rearrange("p m t (j r) -> p m j r t", r=2)
-    nc.vector.tensor_scalar_mul(out=partner[:, :, :, 0, :], in0=pairs[:, :, :, 1, :], scalar1=-1.0)
-    nc.vector.tensor_copy(out=partner[:, :, :, 1, :], in_=pairs[:, :, :, 0, :])
-    nc.vector.tensor_copy(out=grouped[:, ROT:W_COLS, :], in_=raw[:, 2].rearrange("p t c -> p c t"))
+    for cols, r in ((B_COLS, 1), (A_COLS, 0)):
+        for m in range(2):
+            nc.vector.tensor_copy(
+                out=grouped[:, cols.start + m * QD // 2 : cols.start + (m + 1) * QD // 2, :],
+                in_=raw[:, m].rearrange("p t (c r) -> p r c t", r=2)[:, r],
+            )
+    nc.vector.tensor_copy(out=grouped[:, V_COLS, :], in_=raw[:, 2].rearrange("p t c -> p c t"))
 
     codes = consts.tile([P, W_COLS], U32, align_bytes=64)
     scales = consts.tile([P, W_COLS], U8, align_bytes=64)
-    for cols in (slice(0, ROT), slice(ROT, W_COLS)):
+    for cols in (BA_COLS, V_COLS):
         nc.vector.quantize_mx(
             out=codes[:, cols].bitcast(FP8X4),
             scales=scales[:, cols],
@@ -122,10 +131,11 @@ def tile_flexattentionblock_pa_t_kernel(tc, x, attn_norm_w, wq, wk, wv, out_0, o
         setup = ctx.enter_context(tc.tile_pool(name="setup", bufs=1))
         resident = ctx.enter_context(tc.tile_pool(name="resident", bufs=1))
         stream = ctx.enter_context(tc.tile_pool(name="stream", bufs=3))
-        per_tile = ctx.enter_context(tc.tile_pool(name="per_tile", bufs=GROUP))
+        per_tile = ctx.enter_context(tc.tile_pool(name="per_tile", bufs=4))
         psum_gain = ctx.enter_context(tc.psum_pool(name="psum_gain", bufs=1))
         psum_t = ctx.enter_context(tc.psum_pool(name="psum_t", bufs=2))
-        psum_rot = ctx.enter_context(tc.psum_pool(name="psum_rot", bufs=GROUP))
+        psum_ba = ctx.enter_context(tc.psum_pool(name="psum_ba", bufs=GROUP // PAIR))
+        psum_sum = ctx.enter_context(tc.psum_pool(name="psum_sum", bufs=1))
         psum_v = ctx.enter_context(tc.psum_pool(name="psum_v", bufs=1))
         ctx.enter_context(tc.manual_schedule())
 
@@ -161,7 +171,7 @@ def tile_flexattentionblock_pa_t_kernel(tc, x, attn_norm_w, wq, wk, wv, out_0, o
         w_codes, w_scales = quantise_weights(nc, consts, setup, w_raw)
 
         squares_of, rstd_of, h_of, grouped_of, codes_of = {}, {}, {}, {}, {}
-        v_bank_of, rot_banks_of = {}, {}
+        v_bank_of, ba_banks_of, sum_bank_of = {}, {}, {}
 
         def sum_squares(n, half):
             if half == 0:
@@ -218,33 +228,35 @@ def tile_flexattentionblock_pa_t_kernel(tc, x, attn_norm_w, wq, wk, wv, out_0, o
             )
             codes_of[n] = (h_codes, h_scales)
 
-        def project_v(n):
+        def project(n, t, out, w_cols, start, stop):
             h_codes, h_scales = codes_of[n]
+            cols = slice(t * P, (t + 1) * P)
+            nc.tensor.matmul_mx(
+                out=out,
+                lhsT=h_codes[:, cols].bitcast(FP8X4), lhsT_scale=h_scales[:, cols],
+                rhs=w_codes[:, w_cols].bitcast(FP8X4), rhs_scale=w_scales[:, w_cols],
+                start=start, stop=stop,
+            )
+
+        def project_v(n):
             v_ps = psum_v.tile([P, GROUP, QD], F32)
             for t in range(GROUP):
-                cols = slice(t * P, (t + 1) * P)
-                nc.tensor.matmul_mx(
-                    out=v_ps[:, t, :],
-                    lhsT=h_codes[:, cols].bitcast(FP8X4), lhsT_scale=h_scales[:, cols],
-                    rhs=w_codes[:, ROT:W_COLS].bitcast(FP8X4), rhs_scale=w_scales[:, ROT:W_COLS],
-                    start=True, stop=True,
-                )
+                project(n, t, v_ps[:, t, :], V_COLS, True, True)
             v_bank_of[n] = v_ps
 
         def project_rot(n):
-            h_codes, h_scales = codes_of[n]
-            rot_banks = []
+            sum_ps = psum_sum.tile([P, GROUP, HALF], F32)
             for t in range(GROUP):
-                cols = slice(t * P, (t + 1) * P)
-                rot_ps = psum_rot.tile([P, ROT], F32)
-                nc.tensor.matmul_mx(
-                    out=rot_ps[:],
-                    lhsT=h_codes[:, cols].bitcast(FP8X4), lhsT_scale=h_scales[:, cols],
-                    rhs=w_codes[:, 0:ROT].bitcast(FP8X4), rhs_scale=w_scales[:, 0:ROT],
-                    start=True, stop=True,
-                )
-                rot_banks.append(rot_ps)
-            rot_banks_of[n] = rot_banks
+                project(n, t, sum_ps[:, t, :], B_COLS, True, False)
+                project(n, t, sum_ps[:, t, :], A_COLS, False, True)
+            sum_bank_of[n] = sum_ps
+            ba_banks = []
+            for t in range(0, GROUP, PAIR):
+                ba_ps = psum_ba.tile([P, PAIR, 2 * HALF], F32)
+                for s in range(PAIR):
+                    project(n, t + s, ba_ps[:, s, :], BA_COLS, True, True)
+                ba_banks.append(ba_ps)
+            ba_banks_of[n] = ba_banks
 
         def store(n, dram, sb):
             b, g = divmod(n, GROUPS)
@@ -260,19 +272,36 @@ def tile_flexattentionblock_pa_t_kernel(tc, x, attn_norm_w, wq, wk, wv, out_0, o
 
         def rotate_and_store(n):
             first_tile = (n % GROUPS) * GROUP
-            rotated = stream.tile([P, 2 * HEADS, GROUP, HEAD_DIM], F32)
-            for t in range(GROUP):
-                products = per_tile.tile([P, 2, 2 * HEADS, HEAD_DIM], F32)
+            rotated = stream.tile([P, ROT_HEADS, GROUP, HEAD_DIM], F32)
+            shared = stream.tile([P, GROUP, ROT_HEADS, PAIRS], F32)
+            nc.vector.tensor_tensor(
+                out=shared[:],
+                in0=sum_bank_of[n][:].rearrange("p t (m j) -> p t m j", m=ROT_HEADS),
+                in1=cos_table[:, first_tile : first_tile + GROUP].unsqueeze(2).to_broadcast(
+                    [P, GROUP, ROT_HEADS, PAIRS]
+                ),
+                op=ALU.mult,
+            )
+            for half in range(GROUP // PAIR):
+                swing = stream.tile([P, PAIR, HALF, 2], F32)
+                tiles = slice(first_tile + half * PAIR, first_tile + (half + 1) * PAIR)
                 nc.vector.tensor_tensor(
-                    out=products[:],
-                    in0=rot_banks_of[n][t][:].rearrange("p (c r d) -> p c r d", c=2, r=2 * HEADS),
-                    in1=table[:, first_tile + t].unsqueeze(2).to_broadcast(
-                        [P, 2, 2 * HEADS, HEAD_DIM]
+                    out=swing[:].rearrange("p t (m j) r -> p t m (j r)", m=ROT_HEADS),
+                    in0=ba_banks_of[n][half][:].rearrange(
+                        "p t (r m j) -> p t m j r", r=2, m=ROT_HEADS
                     ),
+                    in1=swing_table[:, tiles].rearrange("p t j r -> p t (j r)").unsqueeze(2)
+                    .to_broadcast([P, PAIR, ROT_HEADS, 2 * PAIRS]),
                     op=ALU.mult,
                 )
+                part = slice(half * PAIR, (half + 1) * PAIR)
                 nc.gpsimd.tensor_tensor(
-                    out=rotated[:, :, t, :], in0=products[:, 0], in1=products[:, 1], op=ALU.add
+                    out=rotated[:, :, part, :].rearrange("p m t d -> p t m d"),
+                    in0=swing[:].rearrange("p t (m j) r -> p t m (j r)", m=ROT_HEADS),
+                    in1=shared[:, part].unsqueeze(4).to_broadcast(
+                        [P, PAIR, ROT_HEADS, PAIRS, 2]
+                    ),
+                    op=ALU.add,
                 )
             store(n, out_0, rotated[:, 0:HEADS])
             store(n, out_1, rotated[:, HEADS:])
@@ -281,7 +310,7 @@ def tile_flexattentionblock_pa_t_kernel(tc, x, attn_norm_w, wq, wk, wv, out_0, o
             sum_squares(n, 0)
             sum_squares(n, 1)
             finish_rstd(n)
-        table = rotation_table(nc, consts, setup, turns)
+        cos_table, swing_table = rotation_tables(nc, consts, setup, turns)
 
         for n in range(n_groups + 2):
             ahead, behind, last = n + 2, n - 1, n - 2

@@ -170,7 +170,7 @@ def tile_flexattentionblock_pa_t_kernel(tc, x, attn_norm_w, wq, wk, wv, out_0, o
         nc.tensor.matmul(out=gain[:], lhsT=ones[:], rhs=gain_row[:], start=True, stop=True)
         w_codes, w_scales = quantise_weights(nc, consts, setup, w_raw)
 
-        squares_of, rstd_of, h_of, grouped_of, codes_of = {}, {}, {}, {}, {}
+        squares_of, rstd_of, h_of, turned_of, grouped_of, codes_of = {}, {}, {}, {}, {}, {}
         v_bank_of, ba_banks_of, sum_bank_of = {}, {}, {}
 
         def sum_squares(n, half):
@@ -214,10 +214,13 @@ def tile_flexattentionblock_pa_t_kernel(tc, x, attn_norm_w, wq, wk, wv, out_0, o
                         in_=words[:, u : 2 * P : 2],
                         identity=identity[:],
                     )
+            turned_of[n, half] = turned
+
+        def group_words(n, half):
             grouped_words = grouped_of[n][:].bitcast(F32).rearrange("p (r u) -> p r u", u=2)
             nc.scalar.copy(
                 out=grouped_words[:, half * 2 * P : (half + 1) * 2 * P, :],
-                in_=turned[:].rearrange("p u r -> p r u"),
+                in_=turned_of[n, half][:].rearrange("p u r -> p r u"),
             )
 
         def quantise(n):
@@ -318,18 +321,19 @@ def tile_flexattentionblock_pa_t_kernel(tc, x, attn_norm_w, wq, wk, wv, out_0, o
                 sum_squares(ahead, 0)
             if n < n_groups:
                 scale_and_turn(n, 0)
-            if 0 <= behind < n_groups:
-                quantise(behind)
             if ahead < n_groups:
                 sum_squares(ahead, 1)
             if n < n_groups:
                 scale_and_turn(n, 1)
+                group_words(n, 0)
+                group_words(n, 1)
             if 0 <= behind < n_groups:
+                quantise(behind)
                 project_v(behind)
                 store_v(behind)
+            if ahead < n_groups:
+                finish_rstd(ahead)
             if last >= 0:
                 rotate_and_store(last)
             if 0 <= behind < n_groups:
                 project_rot(behind)
-            if ahead < n_groups:
-                finish_rstd(ahead)

@@ -33,66 +33,75 @@ W_COLS = 2 * HALF + QD
 
 ROUND_MAGIC = 1.5 * 2.0**23
 TURN_GRID = 2.0**15
+FAST = 8
 
 FLOPS = 2 * BATCH * SEQ * DIM * 3 * QD
 
 
-def rotation_turns(nc, work):
+def start_turns(nc, work):
     position = work.tile([P, TILES], F32)
     nc.gpsimd.iota(
         position[:], pattern=[[1, TILES]], base=0, channel_multiplier=TILES,
         allow_small_or_imprecise_dtypes=True,
     )
-    turns_hi = work.tile([P, TILES, PAIRS], F32)
-    turns_lo = work.tile([P, TILES, PAIRS], F32)
+    turns = work.tile([P, TILES, PAIRS], F32)
+    turns_lo = work.tile([P, TILES, FAST], F32)
     for j in range(PAIRS):
         step = THETA ** (-j / PAIRS) / (2.0 * math.pi)
-        step_hi = round(step * TURN_GRID) / TURN_GRID
-        nc.vector.tensor_scalar_mul(out=turns_hi[:, :, j], in0=position[:], scalar1=step_hi)
-        nc.scalar.mul(out=turns_lo[:, :, j], in_=position[:], mul=step - step_hi)
+        if j < FAST:
+            step_hi = round(step * TURN_GRID) / TURN_GRID
+            nc.vector.tensor_scalar_mul(
+                out=turns_lo[:, :, j], in0=position[:], scalar1=step - step_hi
+            )
+            step = step_hi
+        nc.vector.tensor_scalar_mul(out=turns[:, :, j], in0=position[:], scalar1=step)
+    return turns, turns_lo
 
-    whole = work.tile([P, TILES, PAIRS], F32)
-    nc.vector.tensor_scalar(
-        out=whole[:], in0=turns_hi[:], scalar1=ROUND_MAGIC, scalar2=ROUND_MAGIC,
+
+def take_whole_turns(engine, work, turns):
+    whole = work.tile([P] + list(turns.shape[1:]), F32)
+    engine.tensor_scalar(
+        out=whole[:], in0=turns, scalar1=ROUND_MAGIC, scalar2=ROUND_MAGIC,
         op0=ALU.add, op1=ALU.subtract,
     )
-    nc.vector.tensor_sub(out=turns_hi[:], in0=turns_hi[:], in1=whole[:])
-
-    turns = work.tile([P, 2, TILES, PAIRS], F32)
-    nc.vector.tensor_add(out=turns[:, 0], in0=turns_hi[:], in1=turns_lo[:])
-    nc.vector.tensor_scalar_add(out=turns[:, 1], in0=turns[:, 0], scalar1=0.25)
-    nearest = work.tile([P, 2, TILES, PAIRS], F32)
-    nc.vector.tensor_scalar(
-        out=nearest[:], in0=turns[:], scalar1=ROUND_MAGIC, scalar2=ROUND_MAGIC,
-        op0=ALU.add, op1=ALU.subtract,
-    )
-    nc.vector.tensor_sub(out=turns[:], in0=turns[:], in1=nearest[:])
-    return turns
+    engine.tensor_tensor(out=turns, in0=turns, in1=whole[:], op=ALU.subtract)
 
 
-def rotation_tables(nc, consts, work, turns):
-    size = TILES * PAIRS
+def finish_turns(nc, work, turns, turns_lo):
+    fast = turns[:, :, 0:FAST]
+    nc.gpsimd.tensor_tensor(out=fast, in0=fast, in1=turns_lo[:], op=ALU.add)
+    take_whole_turns(nc.gpsimd, work, fast)
+
+
+def sines(nc, work, turns):
+    signed_sin = work.tile([P, 2, TILES, PAIRS], F32)
+    half_sin = work.tile([P, TILES, PAIRS], F32)
+    half_sin_sq = work.tile([P, TILES, PAIRS], F32)
+    for out, factor in ((half_sin[:], 1.0), (signed_sin[:, 0], -2.0), (signed_sin[:, 1], 2.0)):
+        nc.scalar.activation(out=out, in_=turns[:], func=ACT.Sin, scale=factor * math.pi)
+    nc.scalar.activation(out=half_sin_sq[:], in_=half_sin[:], func=ACT.Square)
+    return signed_sin, half_sin_sq
+
+
+def cosines(nc, consts, work, half_sin_sq):
     cos_table = consts.tile([P, TILES, PAIRS], F32)
-    minus_cos = work.tile([P, size], F32)
-    signed_sin = work.tile([P, 2, size], F32)
-    for out, part, sign in (
-        (cos_table[:].rearrange("p i j -> p (i j)"), 1, 1.0),
-        (minus_cos[:], 1, -1.0),
-        (signed_sin[:, 0], 0, -1.0),
-        (signed_sin[:, 1], 0, 1.0),
-    ):
-        nc.scalar.activation(
-            out=out, in_=turns[:, part].rearrange("p i j -> p (i j)"), func=ACT.Sin,
-            scale=sign * 2.0 * math.pi,
+    minus_cos = work.tile([P, TILES, PAIRS], F32)
+    for out, sign in ((cos_table, 1.0), (minus_cos, -1.0)):
+        nc.gpsimd.tensor_scalar(
+            out=out[:], in0=half_sin_sq[:], scalar1=-2.0 * sign, scalar2=sign,
+            op0=ALU.mult, op1=ALU.add,
         )
-    swing_table = consts.tile([P, TILES, PAIRS, 2], F32)
+    return cos_table, minus_cos
+
+
+def swing_part(nc, swing_table, minus_cos, signed_sin, tiles):
+    shape = [P, tiles.stop - tiles.start, PAIRS, 2]
     nc.gpsimd.tensor_tensor(
-        out=swing_table[:].rearrange("p i j r -> p (i j) r"),
-        in0=minus_cos[:].unsqueeze(2).to_broadcast([P, size, 2]),
-        in1=signed_sin[:].rearrange("p r n -> p n r"),
+        out=swing_table[:, tiles],
+        in0=minus_cos[:, tiles].unsqueeze(3).to_broadcast(shape),
+        in1=signed_sin[:, :, tiles].rearrange("p r i j -> p i j r"),
         op=ALU.add,
     )
-    return cos_table, swing_table
 
 
 def load_weights(nc, work, wq, wk, wv):
@@ -150,15 +159,20 @@ def tile_flexattentionblock_pa_t_kernel(tc, x, attn_norm_w, wq, wk, wv, out_0, o
             tokens = x[b].rearrange("(p i) k -> p i k", i=TILES)
             for g in range(GROUPS):
                 x_sb = resident.tile([P, GROUP, DIM], BF16, name="x_%d_%d" % (b, g))
-                nc.sync.dma_start(out=x_sb[:], in_=tokens[:, g * GROUP : (g + 1) * GROUP, :])
+                step = 1 if b == 0 and g < 2 else GROUP
+                for t in range(0, GROUP, step):
+                    i = g * GROUP + t
+                    nc.sync.dma_start(
+                        out=x_sb[:, t : t + step, :], in_=tokens[:, i : i + step, :]
+                    )
                 x_groups.append(x_sb)
-                if b == 0 and g == 0:
+                if b == 0 and g == 1:
                     nc.sync.dma_start(
                         out=gain_row[0:1, :], in_=attn_norm_w.rearrange("(o k) -> o k", o=1)
                     )
                     w_raw = load_weights(nc, setup, wq, wk, wv)
 
-        turns = rotation_turns(nc, setup)
+        turns, turns_lo = start_turns(nc, setup)
         identity = consts.tile([P, P], F32)
         masks.make_identity(nc, identity[:])
         minus_half = consts.tile([P, GROUP], F32)
@@ -168,21 +182,26 @@ def tile_flexattentionblock_pa_t_kernel(tc, x, attn_norm_w, wq, wk, wv, out_0, o
         nc.vector.memset(ones[:], 1.0)
         gain = psum_gain.tile([P, DIM], F32)
         nc.tensor.matmul(out=gain[:], lhsT=ones[:], rhs=gain_row[:], start=True, stop=True)
-        w_codes, w_scales = quantise_weights(nc, consts, setup, w_raw)
 
         squares_of, rstd_of, h_of, turned_of, grouped_of, codes_of = {}, {}, {}, {}, {}, {}
         v_bank_of, ba_banks_of, sum_bank_of = {}, {}, {}
 
-        def sum_squares(n, half):
+        def sum_squares(n, half, on_vector=False):
             if half == 0:
                 squares = stream.tile([P, GROUP], F32)
                 squares_of[n] = squares
             for t in (2 * half, 2 * half + 1):
+                x_tile, total = x_groups[n][:, t, :], squares_of[n][:, t : t + 1]
                 unread = per_tile.tile([P, DIM], BF16)
-                nc.scalar.activation(
-                    out=unread[:], in_=x_groups[n][:, t, :], func=ACT.Square,
-                    accum_out=squares_of[n][:, t : t + 1],
-                )
+                if on_vector:
+                    nc.vector.scalar_tensor_tensor(
+                        out=unread[:], in0=x_tile, scalar=1.0, in1=x_tile,
+                        op0=ALU.mult, op1=ALU.mult, accum_out=total,
+                    )
+                else:
+                    nc.scalar.activation(
+                        out=unread[:], in_=x_tile, func=ACT.Square, accum_out=total
+                    )
 
         def finish_rstd(n):
             mean_sq = stream.tile([P, GROUP], F32)
@@ -298,7 +317,8 @@ def tile_flexattentionblock_pa_t_kernel(tc, x, attn_norm_w, wq, wk, wv, out_0, o
                     op=ALU.mult,
                 )
                 part = slice(half * PAIR, (half + 1) * PAIR)
-                nc.gpsimd.tensor_tensor(
+                adder = nc.gpsimd if n < n_groups - 1 else nc.vector
+                adder.tensor_tensor(
                     out=rotated[:, :, part, :].rearrange("p m t d -> p t m d"),
                     in0=swing[:].rearrange("p t (m j) r -> p t m (j r)", m=ROT_HEADS),
                     in1=shared[:, part].unsqueeze(4).to_broadcast(
@@ -309,30 +329,44 @@ def tile_flexattentionblock_pa_t_kernel(tc, x, attn_norm_w, wq, wk, wv, out_0, o
             store(n, out_0, rotated[:, 0:HEADS])
             store(n, out_1, rotated[:, HEADS:])
 
-        for n in range(2):
-            sum_squares(n, 0)
-            sum_squares(n, 1)
-            finish_rstd(n)
-        cos_table, swing_table = rotation_tables(nc, consts, setup, turns)
+        sum_squares(0, 0)
+        sum_squares(0, 1, on_vector=True)
+        finish_rstd(0)
+        take_whole_turns(nc.vector, setup, turns[:])
+        finish_turns(nc, setup, turns, turns_lo)
+        sum_squares(1, 0)
+        sum_squares(1, 1, on_vector=True)
+        finish_rstd(1)
+        sum_squares(2, 0)
+        sum_squares(2, 1)
+        finish_rstd(2)
+        signed_sin, half_sin_sq = sines(nc, setup, turns)
+        cos_table, minus_cos = cosines(nc, consts, setup, half_sin_sq)
+        swing_table = consts.tile([P, TILES, PAIRS, 2], F32)
 
         for n in range(n_groups + 2):
             ahead, behind, last = n + 2, n - 1, n - 2
-            if ahead < n_groups:
+            if 2 < ahead < n_groups:
                 sum_squares(ahead, 0)
             if n < n_groups:
                 scale_and_turn(n, 0)
-            if ahead < n_groups:
+            if 2 < ahead < n_groups:
                 sum_squares(ahead, 1)
             if n < n_groups:
                 scale_and_turn(n, 1)
                 group_words(n, 0)
                 group_words(n, 1)
+            if n == 0:
+                w_codes, w_scales = quantise_weights(nc, consts, setup, w_raw)
             if 0 <= behind < n_groups:
                 quantise(behind)
                 project_v(behind)
                 store_v(behind)
-            if ahead < n_groups:
+            if 2 < ahead < n_groups:
                 finish_rstd(ahead)
+            if n < GROUPS:
+                tiles = slice(n * GROUP, (n + 1) * GROUP)
+                swing_part(nc, swing_table, minus_cos, signed_sin, tiles)
             if last >= 0:
                 rotate_and_store(last)
             if 0 <= behind < n_groups:

@@ -177,6 +177,11 @@ def tile_flexattentionblock_pa_t_kernel(tc, x, attn_norm_w, wq, wk, wv, out_0, o
         masks.make_identity(nc, identity[:])
         minus_half = consts.tile([P, GROUP], F32)
         nc.gpsimd.memset(minus_half[:], -0.5)
+        eps_col = consts.tile([P, 1], F32)
+        nc.gpsimd.tensor_scalar(
+            out=eps_col[:], in0=minus_half[:, 0:1], scalar1=0.0, scalar2=EPS,
+            op0=ALU.mult, op1=ALU.add,
+        )
 
         ones = setup.tile([P, P], BF16)
         nc.vector.memset(ones[:], 1.0)
@@ -204,6 +209,14 @@ def tile_flexattentionblock_pa_t_kernel(tc, x, attn_norm_w, wq, wk, wv, out_0, o
                     )
 
         def finish_rstd(n):
+            rstd = stream.tile([P, GROUP], F32)
+            nc.scalar.activation(
+                out=rstd[:], in_=squares_of[n][:], func=ACT.Abs_reciprocal_sqrt,
+                scale=1.0 / DIM, bias=eps_col[:],
+            )
+            rstd_of[n] = rstd
+
+        def finish_first_rstd(n):
             mean_sq = stream.tile([P, GROUP], F32)
             nc.gpsimd.tensor_scalar(
                 out=mean_sq[:], in0=squares_of[n][:], scalar1=1.0 / DIM, scalar2=EPS,
@@ -331,15 +344,15 @@ def tile_flexattentionblock_pa_t_kernel(tc, x, attn_norm_w, wq, wk, wv, out_0, o
 
         sum_squares(0, 0)
         sum_squares(0, 1, on_vector=True)
-        finish_rstd(0)
+        finish_first_rstd(0)
         take_whole_turns(nc.vector, setup, turns[:])
         finish_turns(nc, setup, turns, turns_lo)
         sum_squares(1, 0)
         sum_squares(1, 1, on_vector=True)
-        finish_rstd(1)
+        finish_first_rstd(1)
         sum_squares(2, 0)
         sum_squares(2, 1)
-        finish_rstd(2)
+        finish_first_rstd(2)
         signed_sin, half_sin_sq = sines(nc, setup, turns)
         cos_table, minus_cos = cosines(nc, consts, setup, half_sin_sq)
         swing_table = consts.tile([P, TILES, PAIRS, 2], F32)
@@ -352,6 +365,8 @@ def tile_flexattentionblock_pa_t_kernel(tc, x, attn_norm_w, wq, wk, wv, out_0, o
                 scale_and_turn(n, 0)
             if 2 < ahead < n_groups:
                 sum_squares(ahead, 1)
+            if 2 < ahead < n_groups:
+                finish_rstd(ahead)
             if n < n_groups:
                 scale_and_turn(n, 1)
                 group_words(n, 0)
@@ -362,8 +377,6 @@ def tile_flexattentionblock_pa_t_kernel(tc, x, attn_norm_w, wq, wk, wv, out_0, o
                 quantise(behind)
                 project_v(behind)
                 store_v(behind)
-            if 2 < ahead < n_groups:
-                finish_rstd(ahead)
             if n < GROUPS:
                 tiles = slice(n * GROUP, (n + 1) * GROUP)
                 swing_part(nc, swing_table, minus_cos, signed_sin, tiles)

@@ -26,6 +26,7 @@ PACK = 4
 TILES = SEQ // P
 GROUP = 4
 GROUPS = TILES // GROUP
+SCALAR_TILE, SCALAR_GROUPS = 3, (4, 7, 10, 13, 14, 15)
 PAIR = 2
 B_COLS, A_COLS, V_COLS = slice(0, HALF), slice(HALF, 2 * HALF), slice(2 * HALF, 2 * HALF + QD)
 BA_COLS = slice(0, 2 * HALF)
@@ -187,9 +188,11 @@ def tile_flexattentionblock_pa_t_kernel(tc, x, attn_norm_w, wq, wk, wv, out_0, o
         nc.vector.memset(ones[:], 1.0)
         gain = psum_gain.tile([P, DIM], F32)
         nc.tensor.matmul(out=gain[:], lhsT=ones[:], rhs=gain_row[:], start=True, stop=True)
+        gain_sb = consts.tile([P, DIM], F32)
 
         squares_of, rstd_of, h_of, turned_of, grouped_of, codes_of = {}, {}, {}, {}, {}, {}
-        v_bank_of, ba_banks_of, sum_bank_of = {}, {}, {}
+        x_gain_of = {}
+        v_bank_of, ba_banks_of, sum_bank_of, shared_of, swing_of = {}, {}, {}, {}, {}
 
         def sum_squares(n, half, on_vector=False):
             if half == 0:
@@ -226,13 +229,30 @@ def tile_flexattentionblock_pa_t_kernel(tc, x, attn_norm_w, wq, wk, wv, out_0, o
             nc.gpsimd.tensor_tensor(out=rstd[:], in0=mean_sq[:], in1=minus_half[:], op=ALU.pow)
             rstd_of[n] = rstd
 
+        def multiply_by_gain(n):
+            x_gain = stream.tile([P, DIM], F32)
+            nc.gpsimd.tensor_tensor(
+                out=x_gain[:], in0=x_groups[n][:, SCALAR_TILE, :], in1=gain_sb[:], op=ALU.mult
+            )
+            x_gain_of[n] = x_gain
+
+        def new_h(n):
+            h_of[n] = stream.tile([P, GROUP, DIM], BF16, name="h")
+
+        def scale_on_scalar(n):
+            nc.scalar.activation(
+                out=h_of[n][:, SCALAR_TILE, :], in_=x_gain_of[n][:], func=ACT.Copy,
+                scale=rstd_of[n][:, SCALAR_TILE : SCALAR_TILE + 1],
+            )
+
         def scale_and_turn(n, half):
             if half == 0:
-                h = stream.tile([P, GROUP, DIM], BF16)
                 grouped = stream.tile([P, GROUP * P * PACK], BF16, align_bytes=64)
-                h_of[n], grouped_of[n] = h, grouped
+                grouped_of[n] = grouped
             h = h_of[n]
             for t in (2 * half, 2 * half + 1):
+                if n in x_gain_of and t == SCALAR_TILE:
+                    continue
                 nc.vector.scalar_tensor_tensor(
                     out=h[:, t, :], in0=x_groups[n][:, t, :], scalar=rstd_of[n][:, t : t + 1],
                     in1=gain[:], op0=ALU.mult, op1=ALU.mult,
@@ -305,10 +325,10 @@ def tile_flexattentionblock_pa_t_kernel(tc, x, attn_norm_w, wq, wk, wv, out_0, o
             )
             store(n, out_2, v_sb[:])
 
-        def rotate_and_store(n):
+        def rotate_shared(n):
             first_tile = (n % GROUPS) * GROUP
-            rotated = stream.tile([P, ROT_HEADS, GROUP, HEAD_DIM], F32)
             shared = stream.tile([P, GROUP, ROT_HEADS, PAIRS], F32)
+            shared_of[n] = shared
             nc.vector.tensor_tensor(
                 out=shared[:],
                 in0=sum_bank_of[n][:].rearrange("p t (m j) -> p t m j", m=ROT_HEADS),
@@ -317,24 +337,28 @@ def tile_flexattentionblock_pa_t_kernel(tc, x, attn_norm_w, wq, wk, wv, out_0, o
                 ),
                 op=ALU.mult,
             )
+
+        def rotate_swing(n, half):
+            first = (n % GROUPS) * GROUP + half * PAIR
+            swing = stream.tile([P, PAIR, HALF, 2], F32)
+            swing_of[n, half] = swing
+            nc.vector.tensor_tensor(
+                out=swing[:].rearrange("p t (m j) r -> p t m (j r)", m=ROT_HEADS),
+                in0=ba_banks_of[n][half][:].rearrange("p t (r m j) -> p t m j r", r=2, m=ROT_HEADS),
+                in1=swing_table[:, first : first + PAIR].rearrange("p t j r -> p t (j r)")
+                .unsqueeze(2).to_broadcast([P, PAIR, ROT_HEADS, 2 * PAIRS]),
+                op=ALU.mult,
+            )
+
+        def finish_rotation(n):
+            rotated = stream.tile([P, ROT_HEADS, GROUP, HEAD_DIM], F32)
+            adder = nc.gpsimd if n < n_groups - 1 else nc.vector
             for half in range(GROUP // PAIR):
-                swing = stream.tile([P, PAIR, HALF, 2], F32)
-                tiles = slice(first_tile + half * PAIR, first_tile + (half + 1) * PAIR)
-                nc.vector.tensor_tensor(
-                    out=swing[:].rearrange("p t (m j) r -> p t m (j r)", m=ROT_HEADS),
-                    in0=ba_banks_of[n][half][:].rearrange(
-                        "p t (r m j) -> p t m j r", r=2, m=ROT_HEADS
-                    ),
-                    in1=swing_table[:, tiles].rearrange("p t j r -> p t (j r)").unsqueeze(2)
-                    .to_broadcast([P, PAIR, ROT_HEADS, 2 * PAIRS]),
-                    op=ALU.mult,
-                )
                 part = slice(half * PAIR, (half + 1) * PAIR)
-                adder = nc.gpsimd if n < n_groups - 1 else nc.vector
                 adder.tensor_tensor(
                     out=rotated[:, :, part, :].rearrange("p m t d -> p t m d"),
-                    in0=swing[:].rearrange("p t (m j) r -> p t m (j r)", m=ROT_HEADS),
-                    in1=shared[:, part].unsqueeze(4).to_broadcast(
+                    in0=swing_of[n, half][:].rearrange("p t (m j) r -> p t m (j r)", m=ROT_HEADS),
+                    in1=shared_of[n][:, part].unsqueeze(4).to_broadcast(
                         [P, PAIR, ROT_HEADS, PAIRS, 2]
                     ),
                     op=ALU.add,
@@ -348,6 +372,7 @@ def tile_flexattentionblock_pa_t_kernel(tc, x, attn_norm_w, wq, wk, wv, out_0, o
         take_whole_turns(nc.vector, setup, turns[:])
         finish_turns(nc, setup, turns, turns_lo)
         sum_squares(1, 0)
+        nc.scalar.copy(out=gain_sb[:], in_=gain[:])
         sum_squares(1, 1, on_vector=True)
         finish_first_rstd(1)
         sum_squares(2, 0)
@@ -359,28 +384,37 @@ def tile_flexattentionblock_pa_t_kernel(tc, x, attn_norm_w, wq, wk, wv, out_0, o
 
         for n in range(n_groups + 2):
             ahead, behind, last = n + 2, n - 1, n - 2
+            scaling, producing = n < n_groups, 0 <= behind < n_groups
+            if scaling:
+                new_h(n)
+                if n in x_gain_of:
+                    scale_on_scalar(n)
             if 2 < ahead < n_groups:
                 sum_squares(ahead, 0)
-            if n < n_groups:
-                scale_and_turn(n, 0)
-            if 2 < ahead < n_groups:
                 sum_squares(ahead, 1)
-            if 2 < ahead < n_groups:
                 finish_rstd(ahead)
-            if n < n_groups:
+            if scaling:
+                scale_and_turn(n, 0)
                 scale_and_turn(n, 1)
                 group_words(n, 0)
                 group_words(n, 1)
             if n == 0:
                 w_codes, w_scales = quantise_weights(nc, consts, setup, w_raw)
-            if 0 <= behind < n_groups:
+            if last >= 0:
+                store_v(last)
+                rotate_shared(last)
+                rotate_swing(last, 0)
+            if producing:
                 quantise(behind)
-                project_v(behind)
-                store_v(behind)
             if n < GROUPS:
                 tiles = slice(n * GROUP, (n + 1) * GROUP)
                 swing_part(nc, swing_table, minus_cos, signed_sin, tiles)
             if last >= 0:
-                rotate_and_store(last)
-            if 0 <= behind < n_groups:
+                rotate_swing(last, 1)
+            if n + 1 in SCALAR_GROUPS:
+                multiply_by_gain(n + 1)
+            if last >= 0:
+                finish_rotation(last)
+            if producing:
                 project_rot(behind)
+                project_v(behind)

import math
from contextlib import ExitStack

import concourse.masks as masks
import concourse.mybir as mybir

F32 = mybir.dt.float32
BF16 = mybir.dt.bfloat16
U32 = mybir.dt.uint32
U8 = mybir.dt.uint8
FP8X4 = mybir.dt.float8_e4m3fn_x4
ALU = mybir.AluOpType
ACT = mybir.ActivationFunctionType

P = 128
BATCH, SEQ, DIM = 4, 2048, 512
HEADS, HEAD_DIM = 2, 64
QD = HEADS * HEAD_DIM
PAIRS = HEAD_DIM // 2
ROT_HEADS = 2 * HEADS
HALF = ROT_HEADS * PAIRS
THETA = 10000.0
EPS = 1e-6

PACK = 4
TILES = SEQ // P
GROUP = 4
GROUPS = TILES // GROUP
SCALAR_TILE, SCALAR_GROUPS = 3, (4, 7, 10, 13, 14, 15)
PAIR = 2
B_COLS, A_COLS, V_COLS = slice(0, HALF), slice(HALF, 2 * HALF), slice(2 * HALF, 2 * HALF + QD)
BA_COLS = slice(0, 2 * HALF)
W_COLS = 2 * HALF + QD

ROUND_MAGIC = 1.5 * 2.0**23
TURN_GRID = 2.0**15
FAST = 8

FLOPS = 2 * BATCH * SEQ * DIM * 3 * QD


def start_turns(nc, work):
    position = work.tile([P, TILES], F32)
    nc.gpsimd.iota(
        position[:], pattern=[[1, TILES]], base=0, channel_multiplier=TILES,
        allow_small_or_imprecise_dtypes=True,
    )
    turns = work.tile([P, TILES, PAIRS], F32)
    turns_lo = work.tile([P, TILES, FAST], F32)
    for j in range(PAIRS):
        step = THETA ** (-j / PAIRS) / (2.0 * math.pi)
        if j < FAST:
            step_hi = round(step * TURN_GRID) / TURN_GRID
            nc.vector.tensor_scalar_mul(
                out=turns_lo[:, :, j], in0=position[:], scalar1=step - step_hi
            )
            step = step_hi
        nc.vector.tensor_scalar_mul(out=turns[:, :, j], in0=position[:], scalar1=step)
    return turns, turns_lo


def take_whole_turns(engine, work, turns):
    whole = work.tile([P] + list(turns.shape[1:]), F32)
    engine.tensor_scalar(
        out=whole[:], in0=turns, scalar1=ROUND_MAGIC, scalar2=ROUND_MAGIC,
        op0=ALU.add, op1=ALU.subtract,
    )
    engine.tensor_tensor(out=turns, in0=turns, in1=whole[:], op=ALU.subtract)


def finish_turns(nc, work, turns, turns_lo):
    fast = turns[:, :, 0:FAST]
    nc.gpsimd.tensor_tensor(out=fast, in0=fast, in1=turns_lo[:], op=ALU.add)
    take_whole_turns(nc.gpsimd, work, fast)


def sines(nc, work, turns):
    signed_sin = work.tile([P, 2, TILES, PAIRS], F32)
    half_sin = work.tile([P, TILES, PAIRS], F32)
    half_sin_sq = work.tile([P, TILES, PAIRS], F32)
    for out, factor in ((half_sin[:], 1.0), (signed_sin[:, 0], -2.0), (signed_sin[:, 1], 2.0)):
        nc.scalar.activation(out=out, in_=turns[:], func=ACT.Sin, scale=factor * math.pi)
    nc.scalar.activation(out=half_sin_sq[:], in_=half_sin[:], func=ACT.Square)
    return signed_sin, half_sin_sq


def cosines(nc, consts, work, half_sin_sq):
    cos_table = consts.tile([P, TILES, PAIRS], F32)
    minus_cos = work.tile([P, TILES, PAIRS], F32)
    for out, sign in ((cos_table, 1.0), (minus_cos, -1.0)):
        nc.gpsimd.tensor_scalar(
            out=out[:], in0=half_sin_sq[:], scalar1=-2.0 * sign, scalar2=sign,
            op0=ALU.mult, op1=ALU.add,
        )
    return cos_table, minus_cos


def swing_part(nc, swing_table, minus_cos, signed_sin, tiles):
    shape = [P, tiles.stop - tiles.start, PAIRS, 2]
    nc.gpsimd.tensor_tensor(
        out=swing_table[:, tiles],
        in0=minus_cos[:, tiles].unsqueeze(3).to_broadcast(shape),
        in1=signed_sin[:, :, tiles].rearrange("p r i j -> p i j r"),
        op=ALU.add,
    )


def load_weights(nc, work, wq, wk, wv):
    raw = work.tile([P, 3, PACK, QD], BF16)
    for m, w in enumerate((wq, wk, wv)):
        nc.sync.dma_start(out=raw[:, m], in_=w.rearrange("(p t) c -> p t c", t=PACK))
    return raw


def quantise_weights(nc, consts, work, raw):
    grouped = work.tile([P, W_COLS, PACK], BF16, align_bytes=64)
    for cols, r in ((B_COLS, 1), (A_COLS, 0)):
        for m in range(2):
            nc.vector.tensor_copy(
                out=grouped[:, cols.start + m * QD // 2 : cols.start + (m + 1) * QD // 2, :],
                in_=raw[:, m].rearrange("p t (c r) -> p r c t", r=2)[:, r],
            )
    nc.vector.tensor_copy(out=grouped[:, V_COLS, :], in_=raw[:, 2].rearrange("p t c -> p c t"))

    codes = consts.tile([P, W_COLS], U32, align_bytes=64)
    scales = consts.tile([P, W_COLS], U8, align_bytes=64)
    for cols in (BA_COLS, V_COLS):
        nc.vector.quantize_mx(
            out=codes[:, cols].bitcast(FP8X4),
            scales=scales[:, cols],
            in_=grouped[:, cols, :].rearrange("p c t -> p (c t)"),
        )
    return codes, scales


def tile_flexattentionblock_pa_t_kernel(tc, x, attn_norm_w, wq, wk, wv, out_0, out_1, out_2):
    nc = tc.nc
    n_groups = BATCH * GROUPS
    with ExitStack() as ctx:
        consts = ctx.enter_context(tc.tile_pool(name="consts", bufs=1))
        setup = ctx.enter_context(tc.tile_pool(name="setup", bufs=1))
        resident = ctx.enter_context(tc.tile_pool(name="resident", bufs=1))
        stream = ctx.enter_context(tc.tile_pool(name="stream", bufs=3))
        per_tile = ctx.enter_context(tc.tile_pool(name="per_tile", bufs=4))
        psum_gain = ctx.enter_context(tc.psum_pool(name="psum_gain", bufs=1))
        psum_t = ctx.enter_context(tc.psum_pool(name="psum_t", bufs=2))
        psum_ba = ctx.enter_context(tc.psum_pool(name="psum_ba", bufs=GROUP // PAIR))
        psum_sum = ctx.enter_context(tc.psum_pool(name="psum_sum", bufs=1))
        psum_v = ctx.enter_context(tc.psum_pool(name="psum_v", bufs=1))
        ctx.enter_context(tc.manual_schedule())

        zero_col = setup.tile([P, 1], F32)
        nc.vector.memset(zero_col[:], 0.0)
        nc.scalar.activation(out=zero_col[:], in_=zero_col[:], func=ACT.Sin)

        gain_row = setup.tile([P, DIM], BF16)
        nc.vector.memset(gain_row[:], 0.0)
        x_groups = []
        for b in range(BATCH):
            tokens = x[b].rearrange("(p i) k -> p i k", i=TILES)
            for g in range(GROUPS):
                x_sb = resident.tile([P, GROUP, DIM], BF16, name="x_%d_%d" % (b, g))
                step = 1 if b == 0 and g < 2 else GROUP
                for t in range(0, GROUP, step):
                    i = g * GROUP + t
                    nc.sync.dma_start(
                        out=x_sb[:, t : t + step, :], in_=tokens[:, i : i + step, :]
                    )
                x_groups.append(x_sb)
                if b == 0 and g == 1:
                    nc.sync.dma_start(
                        out=gain_row[0:1, :], in_=attn_norm_w.rearrange("(o k) -> o k", o=1)
                    )
                    w_raw = load_weights(nc, setup, wq, wk, wv)

        turns, turns_lo = start_turns(nc, setup)
        identity = consts.tile([P, P], F32)
        masks.make_identity(nc, identity[:])
        minus_half = consts.tile([P, GROUP], F32)
        nc.gpsimd.memset(minus_half[:], -0.5)
        eps_col = consts.tile([P, 1], F32)
        nc.gpsimd.tensor_scalar(
            out=eps_col[:], in0=minus_half[:, 0:1], scalar1=0.0, scalar2=EPS,
            op0=ALU.mult, op1=ALU.add,
        )

        ones = setup.tile([P, P], BF16)
        nc.vector.memset(ones[:], 1.0)
        gain = psum_gain.tile([P, DIM], F32)
        nc.tensor.matmul(out=gain[:], lhsT=ones[:], rhs=gain_row[:], start=True, stop=True)
        gain_sb = consts.tile([P, DIM], F32)

        squares_of, rstd_of, h_of, turned_of, grouped_of, codes_of = {}, {}, {}, {}, {}, {}
        x_gain_of = {}
        v_bank_of, ba_banks_of, sum_bank_of, shared_of, swing_of = {}, {}, {}, {}, {}

        def sum_squares(n, half, on_vector=False):
            if half == 0:
                squares = stream.tile([P, GROUP], F32)
                squares_of[n] = squares
            for t in (2 * half, 2 * half + 1):
                x_tile, total = x_groups[n][:, t, :], squares_of[n][:, t : t + 1]
                unread = per_tile.tile([P, DIM], BF16)
                if on_vector:
                    nc.vector.scalar_tensor_tensor(
                        out=unread[:], in0=x_tile, scalar=1.0, in1=x_tile,
                        op0=ALU.mult, op1=ALU.mult, accum_out=total,
                    )
                else:
                    nc.scalar.activation(
                        out=unread[:], in_=x_tile, func=ACT.Square, accum_out=total
                    )

        def finish_rstd(n):
            rstd = stream.tile([P, GROUP], F32)
            nc.scalar.activation(
                out=rstd[:], in_=squares_of[n][:], func=ACT.Abs_reciprocal_sqrt,
                scale=1.0 / DIM, bias=eps_col[:],
            )
            rstd_of[n] = rstd

        def finish_first_rstd(n):
            mean_sq = stream.tile([P, GROUP], F32)
            nc.gpsimd.tensor_scalar(
                out=mean_sq[:], in0=squares_of[n][:], scalar1=1.0 / DIM, scalar2=EPS,
                op0=ALU.mult, op1=ALU.add,
            )
            rstd = stream.tile([P, GROUP], F32)
            nc.gpsimd.tensor_tensor(out=rstd[:], in0=mean_sq[:], in1=minus_half[:], op=ALU.pow)
            rstd_of[n] = rstd

        def multiply_by_gain(n):
            x_gain = stream.tile([P, DIM], F32)
            nc.gpsimd.tensor_tensor(
                out=x_gain[:], in0=x_groups[n][:, SCALAR_TILE, :], in1=gain_sb[:], op=ALU.mult
            )
            x_gain_of[n] = x_gain

        def new_h(n):
            h_of[n] = stream.tile([P, GROUP, DIM], BF16, name="h")

        def scale_on_scalar(n):
            nc.scalar.activation(
                out=h_of[n][:, SCALAR_TILE, :], in_=x_gain_of[n][:], func=ACT.Copy,
                scale=rstd_of[n][:, SCALAR_TILE : SCALAR_TILE + 1],
            )

        def scale_and_turn(n, half):
            if half == 0:
                grouped = stream.tile([P, GROUP * P * PACK], BF16, align_bytes=64)
                grouped_of[n] = grouped
            h = h_of[n]
            for t in (2 * half, 2 * half + 1):
                if n in x_gain_of and t == SCALAR_TILE:
                    continue
                nc.vector.scalar_tensor_tensor(
                    out=h[:, t, :], in0=x_groups[n][:, t, :], scalar=rstd_of[n][:, t : t + 1],
                    in1=gain[:], op0=ALU.mult, op1=ALU.mult,
                )
            turned = psum_t.tile([P, 2, 2 * P], F32)
            for s in range(2):
                words = h[:, 2 * half + s, :].bitcast(F32)
                for u in range(2):
                    nc.tensor.transpose(
                        out=turned[:, u, s * P : (s + 1) * P],
                        in_=words[:, u : 2 * P : 2],
                        identity=identity[:],
                    )
            turned_of[n, half] = turned

        def group_words(n, half):
            grouped_words = grouped_of[n][:].bitcast(F32).rearrange("p (r u) -> p r u", u=2)
            nc.scalar.copy(
                out=grouped_words[:, half * 2 * P : (half + 1) * 2 * P, :],
                in_=turned_of[n, half][:].rearrange("p u r -> p r u"),
            )

        def quantise(n):
            h_codes = stream.tile([P, GROUP * P], U32, align_bytes=64)
            h_scales = stream.tile([P, GROUP * P], U8, align_bytes=64)
            nc.vector.quantize_mx(
                out=h_codes[:].bitcast(FP8X4), scales=h_scales[:], in_=grouped_of[n][:]
            )
            codes_of[n] = (h_codes, h_scales)

        def project(n, t, out, w_cols, start, stop):
            h_codes, h_scales = codes_of[n]
            cols = slice(t * P, (t + 1) * P)
            nc.tensor.matmul_mx(
                out=out,
                lhsT=h_codes[:, cols].bitcast(FP8X4), lhsT_scale=h_scales[:, cols],
                rhs=w_codes[:, w_cols].bitcast(FP8X4), rhs_scale=w_scales[:, w_cols],
                start=start, stop=stop,
            )

        def project_v(n):
            v_ps = psum_v.tile([P, GROUP, QD], F32)
            for t in range(GROUP):
                project(n, t, v_ps[:, t, :], V_COLS, True, True)
            v_bank_of[n] = v_ps

        def project_rot(n):
            sum_ps = psum_sum.tile([P, GROUP, HALF], F32)
            for t in range(GROUP):
                project(n, t, sum_ps[:, t, :], B_COLS, True, False)
                project(n, t, sum_ps[:, t, :], A_COLS, False, True)
            sum_bank_of[n] = sum_ps
            ba_banks = []
            for t in range(0, GROUP, PAIR):
                ba_ps = psum_ba.tile([P, PAIR, 2 * HALF], F32)
                for s in range(PAIR):
                    project(n, t + s, ba_ps[:, s, :], BA_COLS, True, True)
                ba_banks.append(ba_ps)
            ba_banks_of[n] = ba_banks

        def store(n, dram, sb):
            b, g = divmod(n, GROUPS)
            rows = dram[b].rearrange("h (p i) d -> p h i d", i=TILES)
            nc.sync.dma_start(out=rows[:, :, g * GROUP : (g + 1) * GROUP, :], in_=sb)

        def store_v(n):
            v_sb = stream.tile([P, HEADS, GROUP, HEAD_DIM], F32)
            nc.scalar.copy(
                out=v_sb[:], in_=v_bank_of[n][:].rearrange("p t (h d) -> p h t d", h=HEADS)
            )
            store(n, out_2, v_sb[:])

        def rotate_shared(n):
            first_tile = (n % GROUPS) * GROUP
            shared = stream.tile([P, GROUP, ROT_HEADS, PAIRS], F32)
            shared_of[n] = shared
            nc.vector.tensor_tensor(
                out=shared[:],
                in0=sum_bank_of[n][:].rearrange("p t (m j) -> p t m j", m=ROT_HEADS),
                in1=cos_table[:, first_tile : first_tile + GROUP].unsqueeze(2).to_broadcast(
                    [P, GROUP, ROT_HEADS, PAIRS]
                ),
                op=ALU.mult,
            )

        def rotate_swing(n, half):
            first = (n % GROUPS) * GROUP + half * PAIR
            swing = stream.tile([P, PAIR, HALF, 2], F32)
            swing_of[n, half] = swing
            nc.vector.tensor_tensor(
                out=swing[:].rearrange("p t (m j) r -> p t m (j r)", m=ROT_HEADS),
                in0=ba_banks_of[n][half][:].rearrange("p t (r m j) -> p t m j r", r=2, m=ROT_HEADS),
                in1=swing_table[:, first : first + PAIR].rearrange("p t j r -> p t (j r)")
                .unsqueeze(2).to_broadcast([P, PAIR, ROT_HEADS, 2 * PAIRS]),
                op=ALU.mult,
            )

        def finish_rotation(n):
            rotated = stream.tile([P, ROT_HEADS, GROUP, HEAD_DIM], F32)
            adder = nc.gpsimd if n < n_groups - 1 else nc.vector
            for half in range(GROUP // PAIR):
                part = slice(half * PAIR, (half + 1) * PAIR)
                adder.tensor_tensor(
                    out=rotated[:, :, part, :].rearrange("p m t d -> p t m d"),
                    in0=swing_of[n, half][:].rearrange("p t (m j) r -> p t m (j r)", m=ROT_HEADS),
                    in1=shared_of[n][:, part].unsqueeze(4).to_broadcast(
                        [P, PAIR, ROT_HEADS, PAIRS, 2]
                    ),
                    op=ALU.add,
                )
            store(n, out_0, rotated[:, 0:HEADS])
            store(n, out_1, rotated[:, HEADS:])

        sum_squares(0, 0)
        sum_squares(0, 1, on_vector=True)
        finish_first_rstd(0)
        take_whole_turns(nc.vector, setup, turns[:])
        finish_turns(nc, setup, turns, turns_lo)
        sum_squares(1, 0)
        nc.scalar.copy(out=gain_sb[:], in_=gain[:])
        sum_squares(1, 1, on_vector=True)
        finish_first_rstd(1)
        sum_squares(2, 0)
        sum_squares(2, 1)
        finish_first_rstd(2)
        signed_sin, half_sin_sq = sines(nc, setup, turns)
        cos_table, minus_cos = cosines(nc, consts, setup, half_sin_sq)
        swing_table = consts.tile([P, TILES, PAIRS, 2], F32)

        for n in range(n_groups + 2):
            ahead, behind, last = n + 2, n - 1, n - 2
            scaling, producing = n < n_groups, 0 <= behind < n_groups
            if scaling:
                new_h(n)
                if n in x_gain_of:
                    scale_on_scalar(n)
            if 2 < ahead < n_groups:
                sum_squares(ahead, 0)
                sum_squares(ahead, 1)
                finish_rstd(ahead)
            if scaling:
                scale_and_turn(n, 0)
                scale_and_turn(n, 1)
                group_words(n, 0)
                group_words(n, 1)
            if n == 0:
                w_codes, w_scales = quantise_weights(nc, consts, setup, w_raw)
            if last >= 0:
                store_v(last)
                rotate_shared(last)
                rotate_swing(last, 0)
            if producing:
                quantise(behind)
            if n < GROUPS:
                tiles = slice(n * GROUP, (n + 1) * GROUP)
                swing_part(nc, swing_table, minus_cos, signed_sin, tiles)
            if last >= 0:
                rotate_swing(last, 1)
            if n + 1 in SCALAR_GROUPS:
                multiply_by_gain(n + 1)
            if last >= 0:
                finish_rotation(last)
            if producing:
                project_rot(behind)
                project_v(behind)
